import numpy as np
import ml_dtypes


def mxq(x, axis, fmt="e4m3"):
    dtype, down = {"e4m3": (ml_dtypes.float8_e4m3fn, 7), "e5m2": (ml_dtypes.float8_e5m2, 14)}[fmt]
    v = np.moveaxis(np.asarray(x, np.float32).astype(ml_dtypes.bfloat16).astype(np.float64), axis, -1)
    blocks = v.reshape(v.shape[:-1] + (-1, 32))
    amax = np.abs(blocks).max(-1, keepdims=True)
    byte = np.maximum(np.where(amax > 0, np.frexp(amax)[1] - 1 + 127, 0) - down, 1)
    scale = np.exp2(byte - 127.0)
    codes = (blocks / scale).astype(np.float32).astype(dtype).astype(np.float64)
    return np.moveaxis((codes * scale).reshape(v.shape), -1, axis)


WIDE = False


def mx_kscale(k):
    if not WIDE:
        return np.ones(k)
    levels = np.array([10, -10, 5, -5, 0])
    a = np.random.permutation(np.resize(levels, k // 512 * 4)).reshape(k // 512, 4)
    idx = np.arange(k)
    return np.exp2(a[idx // 512, idx % 128 // 32])


BF16 = ml_dtypes.bfloat16


def bf(x):
    return np.asarray(x, np.float32).astype(BF16)


def f64(x):
    return np.asarray(x).astype(np.float64)


B, V, S, N = 128, 512, 64, 128


def setup_inputs():
    s = mx_kscale(V)
    r = s / s.max()
    d = np.random.standard_normal((B, V, S)) * (0.5 + np.random.random_sample((B, 1, S)))
    d = np.copysign(np.sqrt(d * d - np.log(r)[None, :, None]), d)
    return {"fi_v": bf(np.random.standard_normal((B, V, N)) * 0.4 * np.sqrt(V) / r[None, :, None]), "d_av": bf(d)}


def reference(fi_v, d_av):
    w = np.exp(-np.square(f64(d_av)))
    hi = (mxq(w, 1, "e4m3").transpose(0, 2, 1) @ mxq(f64(fi_v), 1, "e4m3")) / fi_v.shape[1]
    wbar = np.mean(w, axis=1)
    out = wbar[:, :, None] * hi
    return out.reshape(out.shape[0], -1)

@@ -1,0 +1,195 @@
+from contextlib import ExitStack
+
+import concourse.mybir as mybir
+from concourse.masks import make_identity
+
+F32 = mybir.dt.float32
+BF16 = mybir.dt.bfloat16
+U32 = mybir.dt.uint32
+U8 = mybir.dt.uint8
+I32 = mybir.dt.int32
+FP8X4 = mybir.dt.float8_e4m3fn_x4
+ACT = mybir.ActivationFunctionType
+
+B, V, S, N = 128, 512, 64, 128
+P = 128
+PACK = 4
+FLOPS = 2 * B * V * S * N
+
+G = 8
+PAIRS = G // 2
+NC = B // G
+HALF = G // 2
+RING = 3
+UNIT = S
+PREFETCH = 3
+
+
+def tile_garnetlayer_kernel(tc, fi_v, d_av, out):
+    nc = tc.nc
+    fi_view = fi_v.rearrange("b (p j) n -> p b (j n)", j=PACK)
+    d_view = d_av.rearrange("b (p j) s -> p b (j s)", j=PACK)
+    out_view = out.rearrange("b (s n) -> (b s) n", n=N).rearrange("(i m) n -> m i n", m=P)
+
+    with ExitStack() as ctx:
+        const = ctx.enter_context(tc.tile_pool(name="const", bufs=1))
+        loads = ctx.enter_context(tc.tile_pool(name="loads", bufs=PREFETCH + 2))
+        work = ctx.enter_context(tc.tile_pool(name="work", bufs=2))
+        keep = ctx.enter_context(tc.tile_pool(name="keep", bufs=3))
+        psum_hi = ctx.enter_context(tc.psum_pool(name="psum_hi", bufs=3))
+        psum_ws = ctx.enter_context(tc.psum_pool(name="psum_ws", bufs=2))
+
+        ident = const.tile([P, P], F32, name="ident")
+        make_identity(nc, ident[:])
+        wq_ring = []
+        wp_ring = []
+        for r in range(RING):
+            wq = const.tile([P, 3 * PAIRS * UNIT], U32, name="wq%d" % r, align_bytes=64)
+            wp = const.tile([P, 3 * PAIRS * UNIT], U8, name="wp%d" % r, align_bytes=64)
+            nc.vector.memset(wq[:].bitcast(I32), 0)
+            nc.vector.memset(wp[:].bitcast(I32), 0)
+            wq_ring.append(wq)
+            wp_ring.append(wp)
+
+        st = {}
+
+        def load(c):
+            d_raw = loads.tile([P, G, PACK * S], BF16, name="d_raw")
+            fi_raw = loads.tile([P, G, PACK * N], BF16, name="fi_raw")
+            for h in range(2):
+                g0 = c * G + h * HALF
+                nc.sync.dma_start(out=d_raw[:, h * HALF:(h + 1) * HALF, :], in_=d_view[:, g0:g0 + HALF, :])
+            for h in range(2):
+                g0 = c * G + h * HALF
+                nc.sync.dma_start(out=fi_raw[:, h * HALF:(h + 1) * HALF, :], in_=fi_view[:, g0:g0 + HALF, :])
+            st[("d_raw", c)] = d_raw
+            st[("fi_raw", c)] = fi_raw
+
+        def weights(c):
+            d_raw = st[("d_raw", c)]
+            dsq = work.tile([P, PACK, G, S], F32, name="dsq")
+            nc.scalar.activation(out=dsq[:], in_=d_raw[:].rearrange("p b (j s) -> p j b s", j=PACK), func=ACT.Square)
+            w32 = keep.tile([P, PACK, G, S], F32, name="w32")
+            nc.scalar.activation(out=w32[:], in_=dsq[:], func=ACT.Exp, scale=-1.0)
+            st[("w32", c)] = w32
+
+        def w_sum(c):
+            w32 = st[("w32", c)]
+            ws = psum_ws.tile([P, PAIRS, P], F32, name="ws")
+            for i in range(PAIRS):
+                for j in range(PACK):
+                    nc.tensor.matmul(
+                        out=ws[:, i, :],
+                        lhsT=w32[:, j, 2 * i:2 * i + 2, :].rearrange("p b s -> p (b s)"),
+                        rhs=ident[:],
+                        is_transpose=True,
+                        start=(j == 0),
+                        stop=(j == PACK - 1),
+                    )
+            st[("ws", c)] = ws
+
+        def w_reduce(c):
+            wsum = keep.tile([P, PAIRS], F32, name="wsum")
+            nc.vector.tensor_reduce(out=wsum[:], in_=st[("ws", c)][:], axis=mybir.AxisListType.X, op=mybir.AluOpType.add)
+            st[("wsum", c)] = wsum
+
+        def fi_tiles(c):
+            st[("fg", c)] = work.tile([P, G, N, PACK], BF16, name="fg", align_bytes=64)
+            st[("fq", c)] = keep.tile([P, G * N], U32, name="fq", align_bytes=64)
+            st[("fp", c)] = keep.tile([P, G * N], U8, name="fp", align_bytes=64)
+
+        def fi_regroup(c, h):
+            fi_raw = st[("fi_raw", c)]
+            fg = st[("fg", c)]
+            gs = slice(h * HALF, (h + 1) * HALF)
+            nc.vector.tensor_copy(
+                out=fg[:, gs].rearrange("p b (c i) t -> p b c t i", i=4),
+                in_=fi_raw[:, gs, :].rearrange("p b (t c i) -> p b c t i", t=PACK, i=4),
+            )
+
+        def fi_quant(c, h):
+            fg = st[("fg", c)]
+            cols = slice(h * HALF * N, (h + 1) * HALF * N)
+            nc.vector.quantize_mx(
+                out=st[("fq", c)][:, cols].bitcast(FP8X4),
+                scales=st[("fp", c)][:, cols],
+                in_=fg[:, h * HALF:(h + 1) * HALF].rearrange("p b n t -> p (b n t)"),
+            )
+
+        def w_cast(c):
+            w32 = st[("w32", c)]
+            wg = work.tile([P, G * S, PACK], BF16, name="wg", align_bytes=64)
+            nc.vector.tensor_copy(
+                out=wg[:].rearrange("p (c i) t -> p c t i", i=4),
+                in_=w32[:].rearrange("p t b s -> p t (b s)").rearrange("p t (c i) -> p c t i", i=4),
+            )
+            st[("wg", c)] = wg
+
+        def w_quant(c):
+            flat = st[("wg", c)][:].rearrange("p c t -> p (c t)")
+            wq = wq_ring[c % RING]
+            wp = wp_ring[c % RING]
+            runs = [(0, 1)] + [(g, g + 2) for g in range(1, G - 1, 2)] + [(G - 1, G)]
+            for lo, hi in runs:
+                unit = 3 * (lo // 2) + 2 * (lo % 2)
+                cols = slice(unit * UNIT, (unit + hi - lo) * UNIT)
+                nc.vector.quantize_mx(
+                    out=wq[:, cols].bitcast(FP8X4),
+                    scales=wp[:, cols],
+                    in_=flat[:, lo * S * PACK:hi * S * PACK],
+                )
+
+        def mx(c):
+            wq = wq_ring[c % RING]
+            wp = wp_ring[c % RING]
+            fq = st[("fq", c)]
+            fp = st[("fp", c)]
+            acc = psum_hi.tile([P, PAIRS * N], F32, name="acc")
+            for i in range(PAIRS):
+                for odd in range(2):
+                    wcols = slice((3 * i + odd) * UNIT, (3 * i + odd + 2) * UNIT)
+                    fcols = slice((2 * i + odd) * N, (2 * i + odd + 1) * N)
+                    nc.tensor.matmul_mx(
+                        out=acc[:, i * N:(i + 1) * N],
+                        lhsT=wq[:, wcols].bitcast(FP8X4),
+                        lhsT_scale=wp[:, wcols],
+                        rhs=fq[:, fcols].bitcast(FP8X4),
+                        rhs_scale=fp[:, fcols],
+                        start=(odd == 0),
+                        stop=(odd == 1),
+                    )
+            st[("acc", c)] = acc
+
+        def finish(c):
+            acc = st[("acc", c)]
+            wbar = keep.tile([P, PAIRS], F32, name="wbar")
+            nc.scalar.mul(out=wbar[:], in_=st[("wsum", c)][:], mul=1.0 / (V * V))
+            res = keep.tile([P, PAIRS, N], F32, name="res")
+            for i in range(PAIRS):
+                nc.scalar.activation(
+                    out=res[:, i, :], in_=acc[:, i * N:(i + 1) * N], func=ACT.Copy, scale=wbar[:, i:i + 1]
+                )
+            nc.gpsimd.dma_start(out=out_view[:, c * PAIRS:(c + 1) * PAIRS, :], in_=res[:])
+
+        ctx.enter_context(tc.manual_schedule())
+        for c in range(PREFETCH):
+            load(c)
+        for t in range(NC + 2):
+            if t + PREFETCH < NC:
+                load(t + PREFETCH)
+            if t < NC:
+                weights(t)
+            c = t - 1
+            if 0 <= c < NC:
+                fi_tiles(c)
+                w_sum(c)
+                fi_regroup(c, 0)
+                w_cast(c)
+                fi_regroup(c, 1)
+                fi_quant(c, 0)
+                w_quant(c)
+                fi_quant(c, 1)
+                w_reduce(c)
+                mx(c)
+            if t >= 2:
+                finish(t - 2)

@@ -18,11 +18,12 @@ FLOPS = 2 * B * V * S * N
 
 G = 8
 PAIRS = G // 2
-NC = B // G
-HALF = G // 2
+PIECE = 4
 RING = 3
 UNIT = S
-PREFETCH = 3
+AHEAD = 6
+SIZES = (2, 2, 4) + (8,) * 14 + (4, 2, 2)
+LATE = 3
 
 
 def tile_garnetlayer_kernel(tc, fi_v, d_av, out):
@@ -30,53 +31,52 @@ def tile_garnetlayer_kernel(tc, fi_v, d_av, out):
     fi_view = fi_v.rearrange("b (p j) n -> p b (j n)", j=PACK)
     d_view = d_av.rearrange("b (p j) s -> p b (j s)", j=PACK)
     out_view = out.rearrange("b (s n) -> (b s) n", n=N).rearrange("(i m) n -> m i n", m=P)
+    nchunks = len(SIZES)
+    starts = [sum(SIZES[:c]) for c in range(nchunks)]
+    assert sum(SIZES) == B
 
     with ExitStack() as ctx:
         const = ctx.enter_context(tc.tile_pool(name="const", bufs=1))
-        loads = ctx.enter_context(tc.tile_pool(name="loads", bufs=PREFETCH + 2))
+        loads = ctx.enter_context(tc.tile_pool(name="loads", bufs=AHEAD + 2))
         work = ctx.enter_context(tc.tile_pool(name="work", bufs=2))
         keep = ctx.enter_context(tc.tile_pool(name="keep", bufs=3))
+        codes = ctx.enter_context(tc.tile_pool(name="codes", bufs=4))
         psum_hi = ctx.enter_context(tc.psum_pool(name="psum_hi", bufs=3))
-        psum_ws = ctx.enter_context(tc.psum_pool(name="psum_ws", bufs=2))
+        psum_ws = ctx.enter_context(tc.psum_pool(name="psum_ws", bufs=3))
 
-        ident = const.tile([P, P], F32, name="ident")
-        make_identity(nc, ident[:])
-        wq_ring = []
-        wp_ring = []
-        for r in range(RING):
-            wq = const.tile([P, 3 * PAIRS * UNIT], U32, name="wq%d" % r, align_bytes=64)
-            wp = const.tile([P, 3 * PAIRS * UNIT], U8, name="wp%d" % r, align_bytes=64)
-            nc.vector.memset(wq[:].bitcast(I32), 0)
-            nc.vector.memset(wp[:].bitcast(I32), 0)
-            wq_ring.append(wq)
-            wp_ring.append(wp)
+        ctx.enter_context(tc.manual_schedule())
 
         st = {}
+
+        def pieces(c):
+            return [(a, min(a + PIECE, SIZES[c])) for a in range(0, SIZES[c], PIECE)]
 
         def load(c):
             d_raw = loads.tile([P, G, PACK * S], BF16, name="d_raw")
             fi_raw = loads.tile([P, G, PACK * N], BF16, name="fi_raw")
-            for h in range(2):
-                g0 = c * G + h * HALF
-                nc.sync.dma_start(out=d_raw[:, h * HALF:(h + 1) * HALF, :], in_=d_view[:, g0:g0 + HALF, :])
-            for h in range(2):
-                g0 = c * G + h * HALF
-                nc.sync.dma_start(out=fi_raw[:, h * HALF:(h + 1) * HALF, :], in_=fi_view[:, g0:g0 + HALF, :])
+            g0 = starts[c]
+            for a, b in pieces(c):
+                nc.sync.dma_start(out=d_raw[:, a:b, :], in_=d_view[:, g0 + a:g0 + b, :])
+            for a, b in pieces(c):
+                nc.sync.dma_start(out=fi_raw[:, a:b, :], in_=fi_view[:, g0 + a:g0 + b, :])
             st[("d_raw", c)] = d_raw
             st[("fi_raw", c)] = fi_raw
 
         def weights(c):
+            ng = SIZES[c]
             d_raw = st[("d_raw", c)]
             dsq = work.tile([P, PACK, G, S], F32, name="dsq")
-            nc.scalar.activation(out=dsq[:], in_=d_raw[:].rearrange("p b (j s) -> p j b s", j=PACK), func=ACT.Square)
+            nc.scalar.activation(
+                out=dsq[:, :, 0:ng, :], in_=d_raw[:, 0:ng, :].rearrange("p b (j s) -> p j b s", j=PACK), func=ACT.Square
+            )
             w32 = keep.tile([P, PACK, G, S], F32, name="w32")
-            nc.scalar.activation(out=w32[:], in_=dsq[:], func=ACT.Exp, scale=-1.0)
+            nc.scalar.activation(out=w32[:, :, 0:ng, :], in_=dsq[:, :, 0:ng, :], func=ACT.Exp, scale=-1.0)
             st[("w32", c)] = w32
 
         def w_sum(c):
             w32 = st[("w32", c)]
             ws = psum_ws.tile([P, PAIRS, P], F32, name="ws")
-            for i in range(PAIRS):
+            for i in range(SIZES[c] // 2):
                 for j in range(PACK):
                     nc.tensor.matmul(
                         out=ws[:, i, :],
@@ -88,48 +88,63 @@ def tile_garnetlayer_kernel(tc, fi_v, d_av, out):
                     )
             st[("ws", c)] = ws
 
-        def w_reduce(c):
-            wsum = keep.tile([P, PAIRS], F32, name="wsum")
-            nc.vector.tensor_reduce(out=wsum[:], in_=st[("ws", c)][:], axis=mybir.AxisListType.X, op=mybir.AluOpType.add)
-            st[("wsum", c)] = wsum
+        def split(c):
+            npairs = SIZES[c] // 2
+            return (npairs + 1) // 2, npairs
+
+        def w_reduce_vector(c):
+            lo, hi = split(c)
+            if lo < hi:
+                wsum = keep.tile([P, PAIRS], F32, name="wsum")
+                nc.vector.tensor_reduce(
+                    out=wsum[:, lo:hi], in_=st[("ws", c)][:, lo:hi, :], axis=mybir.AxisListType.X, op=mybir.AluOpType.add
+                )
+                st[("wsum", c)] = wsum
+
+        def w_reduce_scalar(c):
+            lo, hi = split(c)
+            wbar = keep.tile([P, PAIRS], F32, name="wbar")
+            for i in range(lo):
+                junk = work.tile([P, P], BF16, name="junk")
+                nc.scalar.activation(
+                    out=junk[:], in_=st[("ws", c)][:, i, :], func=ACT.Copy, scale=1.0 / (V * V), accum_out=wbar[:, i:i + 1]
+                )
+            st[("wbar", c)] = wbar
 
         def fi_tiles(c):
             st[("fg", c)] = work.tile([P, G, N, PACK], BF16, name="fg", align_bytes=64)
-            st[("fq", c)] = keep.tile([P, G * N], U32, name="fq", align_bytes=64)
-            st[("fp", c)] = keep.tile([P, G * N], U8, name="fp", align_bytes=64)
+            st[("fq", c)] = codes.tile([P, G * N], U32, name="fq", align_bytes=64)
+            st[("fp", c)] = codes.tile([P, G * N], U8, name="fp", align_bytes=64)
 
-        def fi_regroup(c, h):
-            fi_raw = st[("fi_raw", c)]
-            fg = st[("fg", c)]
-            gs = slice(h * HALF, (h + 1) * HALF)
+        def fi_regroup(c, a, b):
             nc.vector.tensor_copy(
-                out=fg[:, gs].rearrange("p b (c i) t -> p b c t i", i=4),
-                in_=fi_raw[:, gs, :].rearrange("p b (t c i) -> p b c t i", t=PACK, i=4),
+                out=st[("fg", c)][:, a:b].rearrange("p b (c i) t -> p b c t i", i=4),
+                in_=st[("fi_raw", c)][:, a:b, :].rearrange("p b (t c i) -> p b c t i", t=PACK, i=4),
             )
 
-        def fi_quant(c, h):
-            fg = st[("fg", c)]
-            cols = slice(h * HALF * N, (h + 1) * HALF * N)
+        def fi_quant(c, a, b):
+            cols = slice(a * N, b * N)
             nc.vector.quantize_mx(
                 out=st[("fq", c)][:, cols].bitcast(FP8X4),
                 scales=st[("fp", c)][:, cols],
-                in_=fg[:, h * HALF:(h + 1) * HALF].rearrange("p b n t -> p (b n t)"),
+                in_=st[("fg", c)][:, a:b].rearrange("p b n t -> p (b n t)"),
             )
 
         def w_cast(c):
-            w32 = st[("w32", c)]
+            ng = SIZES[c]
             wg = work.tile([P, G * S, PACK], BF16, name="wg", align_bytes=64)
             nc.vector.tensor_copy(
-                out=wg[:].rearrange("p (c i) t -> p c t i", i=4),
-                in_=w32[:].rearrange("p t b s -> p t (b s)").rearrange("p t (c i) -> p c t i", i=4),
+                out=wg[:, 0:ng * S, :].rearrange("p (c i) t -> p c t i", i=4),
+                in_=st[("w32", c)][:, :, 0:ng, :].rearrange("p t b (c i) -> p t b c i", i=4).rearrange("p t b c i -> p (b c) t i"),
             )
             st[("wg", c)] = wg
 
         def w_quant(c):
+            ng = SIZES[c]
             flat = st[("wg", c)][:].rearrange("p c t -> p (c t)")
             wq = wq_ring[c % RING]
             wp = wp_ring[c % RING]
-            runs = [(0, 1)] + [(g, g + 2) for g in range(1, G - 1, 2)] + [(G - 1, G)]
+            runs = [(0, 1)] + [(g, g + 2) for g in range(1, ng - 1, 2)] + [(ng - 1, ng)]
             for lo, hi in runs:
                 unit = 3 * (lo // 2) + 2 * (lo % 2)
                 cols = slice(unit * UNIT, (unit + hi - lo) * UNIT)
@@ -144,13 +159,13 @@ def tile_garnetlayer_kernel(tc, fi_v, d_av, out):
             wp = wp_ring[c % RING]
             fq = st[("fq", c)]
             fp = st[("fp", c)]
-            acc = psum_hi.tile([P, PAIRS * N], F32, name="acc")
-            for i in range(PAIRS):
+            acc = psum_hi.tile([P, PAIRS, N], F32, name="acc")
+            for i in range(SIZES[c] // 2):
                 for odd in range(2):
                     wcols = slice((3 * i + odd) * UNIT, (3 * i + odd + 2) * UNIT)
                     fcols = slice((2 * i + odd) * N, (2 * i + odd + 1) * N)
                     nc.tensor.matmul_mx(
-                        out=acc[:, i * N:(i + 1) * N],
+                        out=acc[:, i, :],
                         lhsT=wq[:, wcols].bitcast(FP8X4),
                         lhsT_scale=wp[:, wcols],
                         rhs=fq[:, fcols].bitcast(FP8X4),
@@ -161,35 +176,57 @@ def tile_garnetlayer_kernel(tc, fi_v, d_av, out):
             st[("acc", c)] = acc
 
         def finish(c):
+            lo, hi = split(c)
             acc = st[("acc", c)]
-            wbar = keep.tile([P, PAIRS], F32, name="wbar")
-            nc.scalar.mul(out=wbar[:], in_=st[("wsum", c)][:], mul=1.0 / (V * V))
+            wbar = st[("wbar", c)]
+            if lo < hi:
+                nc.scalar.mul(out=wbar[:, lo:hi], in_=st[("wsum", c)][:, lo:hi], mul=1.0 / (V * V))
             res = keep.tile([P, PAIRS, N], F32, name="res")
-            for i in range(PAIRS):
-                nc.scalar.activation(
-                    out=res[:, i, :], in_=acc[:, i * N:(i + 1) * N], func=ACT.Copy, scale=wbar[:, i:i + 1]
-                )
-            nc.gpsimd.dma_start(out=out_view[:, c * PAIRS:(c + 1) * PAIRS, :], in_=res[:])
+            for i in range(hi):
+                nc.scalar.activation(out=res[:, i, :], in_=acc[:, i, :], func=ACT.Copy, scale=wbar[:, i:i + 1])
+            queue = nc.sync if c >= nchunks - LATE else nc.gpsimd
+            i0 = starts[c] // 2
+            queue.dma_start(out=out_view[:, i0:i0 + hi, :], in_=res[:, 0:hi, :])
 
-        ctx.enter_context(tc.manual_schedule())
-        for c in range(PREFETCH):
+        for c in range(AHEAD):
             load(c)
-        for t in range(NC + 2):
-            if t + PREFETCH < NC:
-                load(t + PREFETCH)
-            if t < NC:
+
+        ident = const.tile([P, P], F32, name="ident")
+        make_identity(nc, ident[:])
+        wq_ring = []
+        wp_ring = []
+        for r in range(RING):
+            wq = const.tile([P, 3 * PAIRS * UNIT], U32, name="wq%d" % r, align_bytes=64)
+            wp = const.tile([P, 3 * PAIRS * UNIT], U8, name="wp%d" % r, align_bytes=64)
+            nc.vector.memset(wq[:].bitcast(I32), 0)
+            nc.vector.memset(wp[:].bitcast(I32), 0)
+            wq_ring.append(wq)
+            wp_ring.append(wp)
+
+        for t in range(nchunks + 2):
+            if t + AHEAD < nchunks:
+                load(t + AHEAD)
+            if t < nchunks:
                 weights(t)
-            c = t - 1
-            if 0 <= c < NC:
-                fi_tiles(c)
-                w_sum(c)
-                fi_regroup(c, 0)
-                w_cast(c)
-                fi_regroup(c, 1)
-                fi_quant(c, 0)
-                w_quant(c)
-                fi_quant(c, 1)
-                w_reduce(c)
-                mx(c)
+            new = t if t < nchunks else None
+            old = t - 1 if 0 <= t - 1 < nchunks else None
+            if old is not None:
+                w_sum(old)
+                w_reduce_scalar(old)
+            parts = pieces(new) if new is not None else []
+            if new is not None:
+                fi_tiles(new)
+                fi_regroup(new, parts[0][0], parts[0][1])
+            if old is not None:
+                w_cast(old)
+            for a, b in parts[1:]:
+                fi_regroup(new, a, b)
+            if old is not None:
+                w_quant(old)
+            for a, b in parts:
+                fi_quant(new, a, b)
+            if old is not None:
+                w_reduce_vector(old)
+                mx(old)
             if t >= 2:
                 finish(t - 2)

@@ -23,7 +23,7 @@ RING = 3
 UNIT = S
 AHEAD = 6
 SIZES = (2, 2, 4) + (8,) * 14 + (4, 2, 2)
-LATE = 3
+LATE = 20
 
 
 def tile_garnetlayer_kernel(tc, fi_v, d_av, out):

@@ -41,6 +41,7 @@ def tile_garnetlayer_kernel(tc, fi_v, d_av, out):
         work = ctx.enter_context(tc.tile_pool(name="work", bufs=2))
         keep = ctx.enter_context(tc.tile_pool(name="keep", bufs=3))
         codes = ctx.enter_context(tc.tile_pool(name="codes", bufs=4))
+        results = ctx.enter_context(tc.tile_pool(name="results", bufs=8))
         psum_hi = ctx.enter_context(tc.psum_pool(name="psum_hi", bufs=3))
         psum_ws = ctx.enter_context(tc.psum_pool(name="psum_ws", bufs=3))
 
@@ -181,7 +182,7 @@ def tile_garnetlayer_kernel(tc, fi_v, d_av, out):
             wbar = st[("wbar", c)]
             if lo < hi:
                 nc.scalar.mul(out=wbar[:, lo:hi], in_=st[("wsum", c)][:, lo:hi], mul=1.0 / (V * V))
-            res = keep.tile([P, PAIRS, N], F32, name="res")
+            res = results.tile([P, PAIRS, N], F32, name="res")
             for i in range(hi):
                 nc.scalar.activation(out=res[:, i, :], in_=acc[:, i, :], func=ACT.Copy, scale=wbar[:, i:i + 1])
             queue = nc.sync if c >= nchunks - LATE else nc.gpsimd

@@ -96,11 +96,9 @@ def tile_garnetlayer_kernel(tc, fi_v, d_av, out):
         def w_reduce_vector(c):
             lo, hi = split(c)
             if lo < hi:
-                wsum = keep.tile([P, PAIRS], F32, name="wsum")
                 nc.vector.tensor_reduce(
-                    out=wsum[:, lo:hi], in_=st[("ws", c)][:, lo:hi, :], axis=mybir.AxisListType.X, op=mybir.AluOpType.add
+                    out=st[("wbar", c)][:, lo:hi], in_=st[("ws", c)][:, lo:hi, :], axis=mybir.AxisListType.X, op=mybir.AluOpType.add
                 )
-                st[("wsum", c)] = wsum
 
         def w_reduce_scalar(c):
             lo, hi = split(c)
@@ -108,7 +106,7 @@ def tile_garnetlayer_kernel(tc, fi_v, d_av, out):
             for i in range(lo):
                 junk = work.tile([P, P], BF16, name="junk")
                 nc.scalar.activation(
-                    out=junk[:], in_=st[("ws", c)][:, i, :], func=ACT.Copy, scale=1.0 / (V * V), accum_out=wbar[:, i:i + 1]
+                    out=junk[:], in_=st[("ws", c)][:, i, :], func=ACT.Copy, accum_out=wbar[:, i:i + 1]
                 )
             st[("wbar", c)] = wbar
 
@@ -134,9 +132,10 @@ def tile_garnetlayer_kernel(tc, fi_v, d_av, out):
         def w_cast(c):
             ng = SIZES[c]
             wg = work.tile([P, G * S, PACK], BF16, name="wg", align_bytes=64)
-            nc.vector.tensor_copy(
+            nc.vector.tensor_scalar_mul(
                 out=wg[:, 0:ng * S, :].rearrange("p (c i) t -> p c t i", i=4),
-                in_=st[("w32", c)][:, :, 0:ng, :].rearrange("p t b (c i) -> p t b c i", i=4).rearrange("p t b c i -> p (b c) t i"),
+                in0=st[("w32", c)][:, :, 0:ng, :].rearrange("p t b (c i) -> p t b c i", i=4).rearrange("p t b c i -> p (b c) t i"),
+                scalar1=1.0 / (V * V),
             )
             st[("wg", c)] = wg
 
@@ -180,8 +179,6 @@ def tile_garnetlayer_kernel(tc, fi_v, d_av, out):
             lo, hi = split(c)
             acc = st[("acc", c)]
             wbar = st[("wbar", c)]
-            if lo < hi:
-                nc.scalar.mul(out=wbar[:, lo:hi], in_=st[("wsum", c)][:, lo:hi], mul=1.0 / (V * V))
             res = results.tile([P, PAIRS, N], F32, name="res")
             for i in range(hi):
                 nc.scalar.activation(out=res[:, i, :], in_=acc[:, i, :], func=ACT.Copy, scale=wbar[:, i:i + 1])

@@ -91,7 +91,8 @@ def tile_garnetlayer_kernel(tc, fi_v, d_av, out):
 
         def split(c):
             npairs = SIZES[c] // 2
-            return (npairs + 1) // 2, npairs
+            more = 1 if npairs == PAIRS and c % 3 == 0 else 0
+            return (npairs + 1) // 2 + more, npairs
 
         def w_reduce_vector(c):
             lo, hi = split(c)
@@ -196,8 +197,8 @@ def tile_garnetlayer_kernel(tc, fi_v, d_av, out):
         for r in range(RING):
             wq = const.tile([P, 3 * PAIRS * UNIT], U32, name="wq%d" % r, align_bytes=64)
             wp = const.tile([P, 3 * PAIRS * UNIT], U8, name="wp%d" % r, align_bytes=64)
-            nc.vector.memset(wq[:].bitcast(I32), 0)
-            nc.vector.memset(wp[:].bitcast(I32), 0)
+            nc.vector.memset(wq[:].bitcast(I32).rearrange("p (i u w) -> p i u w", u=3, w=UNIT)[:, :, 1, :], 0)
+            nc.vector.memset(wp[:].bitcast(I32).rearrange("p (i u w) -> p i u w", u=3, w=UNIT // 4)[:, :, 1, :], 0)
             wq_ring.append(wq)
             wp_ring.append(wp)
 

@@ -23,7 +23,6 @@ RING = 3
 UNIT = S
 AHEAD = 6
 SIZES = (2, 2, 4) + (8,) * 14 + (4, 2, 2)
-LATE = 20
 
 
 def tile_garnetlayer_kernel(tc, fi_v, d_av, out):
@@ -39,11 +38,13 @@ def tile_garnetlayer_kernel(tc, fi_v, d_av, out):
         const = ctx.enter_context(tc.tile_pool(name="const", bufs=1))
         loads = ctx.enter_context(tc.tile_pool(name="loads", bufs=AHEAD + 2))
         work = ctx.enter_context(tc.tile_pool(name="work", bufs=2))
-        keep = ctx.enter_context(tc.tile_pool(name="keep", bufs=3))
-        codes = ctx.enter_context(tc.tile_pool(name="codes", bufs=4))
+        turned = ctx.enter_context(tc.tile_pool(name="turned", bufs=3))
+        keep = ctx.enter_context(tc.tile_pool(name="keep", bufs=4))
+        codes = ctx.enter_context(tc.tile_pool(name="codes", bufs=6))
         results = ctx.enter_context(tc.tile_pool(name="results", bufs=8))
-        psum_hi = ctx.enter_context(tc.psum_pool(name="psum_hi", bufs=3))
-        psum_ws = ctx.enter_context(tc.psum_pool(name="psum_ws", bufs=3))
+        psum_d = ctx.enter_context(tc.psum_pool(name="psum_d", bufs=4))
+        psum_w = ctx.enter_context(tc.psum_pool(name="psum_w", bufs=2))
+        psum_hi = ctx.enter_context(tc.psum_pool(name="psum_hi", bufs=2))
 
         ctx.enter_context(tc.manual_schedule())
 
@@ -63,53 +64,75 @@ def tile_garnetlayer_kernel(tc, fi_v, d_av, out):
             st[("d_raw", c)] = d_raw
             st[("fi_raw", c)] = fi_raw
 
-        def weights(c):
+        def square(c):
             ng = SIZES[c]
-            d_raw = st[("d_raw", c)]
-            dsq = work.tile([P, PACK, G, S], F32, name="dsq")
+            dsq = turned.tile([P, PACK, G, S], F32, name="dsq")
             nc.scalar.activation(
-                out=dsq[:, :, 0:ng, :], in_=d_raw[:, 0:ng, :].rearrange("p b (j s) -> p j b s", j=PACK), func=ACT.Square
+                out=dsq[:, :, 0:ng, :],
+                in_=st[("d_raw", c)][:, 0:ng, :].rearrange("p b (j s) -> p j b s", j=PACK),
+                func=ACT.Square,
             )
-            w32 = keep.tile([P, PACK, G, S], F32, name="w32")
-            nc.scalar.activation(out=w32[:, :, 0:ng, :], in_=dsq[:, :, 0:ng, :], func=ACT.Exp, scale=-1.0)
-            st[("w32", c)] = w32
+            st[("dsq", c)] = dsq
 
-        def w_sum(c):
-            w32 = st[("w32", c)]
-            ws = psum_ws.tile([P, PAIRS, P], F32, name="ws")
+        def turn(c):
+            dsq = st[("dsq", c)]
             for i in range(SIZES[c] // 2):
+                dt = psum_d.tile([P, PACK, P], F32, name="dt")
                 for j in range(PACK):
-                    nc.tensor.matmul(
-                        out=ws[:, i, :],
-                        lhsT=w32[:, j, 2 * i:2 * i + 2, :].rearrange("p b s -> p (b s)"),
-                        rhs=ident[:],
-                        is_transpose=True,
-                        start=(j == 0),
-                        stop=(j == PACK - 1),
+                    nc.tensor.transpose(
+                        dt[:, j, :], dsq[:, j, 2 * i:2 * i + 2, :].rearrange("p b s -> p (b s)"), ident[:]
                     )
-            st[("ws", c)] = ws
+                st[("dt", c, i)] = dt
 
-        def split(c):
-            npairs = SIZES[c] // 2
-            more = 1 if npairs == PAIRS and c % 3 == 0 else 0
-            return (npairs + 1) // 2 + more, npairs
-
-        def w_reduce_vector(c):
-            lo, hi = split(c)
-            if lo < hi:
-                nc.vector.tensor_reduce(
-                    out=st[("wbar", c)][:, lo:hi], in_=st[("ws", c)][:, lo:hi, :], axis=mybir.AxisListType.X, op=mybir.AluOpType.add
-                )
-
-        def w_reduce_scalar(c):
-            lo, hi = split(c)
-            wbar = keep.tile([P, PAIRS], F32, name="wbar")
-            for i in range(lo):
-                junk = work.tile([P, P], BF16, name="junk")
+        def exp(c):
+            wt = turned.tile([P, PAIRS, 2, P, 2], BF16, name="wt", align_bytes=64)
+            if c % 2 == 0:
+                wsum = keep.tile([P, 2 * PAIRS], F32, name="wsum")
+                wbar = keep.tile([P, 2 * PAIRS], F32, name="wbar")
+                st[("wsum", c // 2)] = wsum
+                st[("wbar", c // 2)] = wbar
+            wsum = st[("wsum", c // 2)]
+            col = first_col(c)
+            for i in range(SIZES[c] // 2):
                 nc.scalar.activation(
-                    out=junk[:], in_=st[("ws", c)][:, i, :], func=ACT.Copy, accum_out=wbar[:, i:i + 1]
+                    out=wt[:, i],
+                    in_=st[("dt", c, i)][:].rearrange("m (h e) q -> m h q e", e=2),
+                    func=ACT.Exp,
+                    scale=-1.0,
+                    accum_out=wsum[:, col + i:col + i + 1],
                 )
-            st[("wbar", c)] = wbar
+            st[("wt", c)] = wt
+
+        def first_col(c):
+            return 0 if c % 2 == 0 else SIZES[c - 1] // 2
+
+        def scale_sums(c):
+            last = c + 1 if c + 1 < nchunks else c
+            used = first_col(last) + SIZES[last] // 2
+            nc.scalar.mul(st[("wbar", c // 2)][:, 0:used], st[("wsum", c // 2)][:, 0:used], 1.0 / (V * V))
+
+        def turn_back(c):
+            wt = st[("wt", c)]
+            npairs = SIZES[c] // 2
+            for k in range(0, npairs, 2):
+                wb = psum_w.tile([P, 2, 2, P], F32, name="wb")
+                for i in range(k, min(k + 2, npairs)):
+                    for h in range(2):
+                        nc.tensor.transpose(
+                            wb[:, i - k, h, :], wt[:, i, h].rearrange("m q e -> m (q e)").bitcast(F32), ident[:]
+                        )
+                st[("wb", c, k)] = wb
+
+        def w_group(c):
+            npairs = SIZES[c] // 2
+            wg = work.tile([P, G * S * PACK], BF16, name="wg", align_bytes=64)
+            words = wg[:].bitcast(F32).rearrange("p (i m h) -> p i m h", m=P, h=2)
+            for k in range(0, npairs, 2):
+                hi = min(k + 2, npairs)
+                nc.vector.tensor_copy(
+                    out=words[:, k:hi], in_=st[("wb", c, k)][:, 0:hi - k].rearrange("p i h m -> p i m h")
+                )
+            st[("wg", c)] = wg
 
         def fi_tiles(c):
             st[("fg", c)] = work.tile([P, G, N, PACK], BF16, name="fg", align_bytes=64)
@@ -130,19 +153,9 @@ def tile_garnetlayer_kernel(tc, fi_v, d_av, out):
                 in_=st[("fg", c)][:, a:b].rearrange("p b n t -> p (b n t)"),
             )
 
-        def w_cast(c):
-            ng = SIZES[c]
-            wg = work.tile([P, G * S, PACK], BF16, name="wg", align_bytes=64)
-            nc.vector.tensor_scalar_mul(
-                out=wg[:, 0:ng * S, :].rearrange("p (c i) t -> p c t i", i=4),
-                in0=st[("w32", c)][:, :, 0:ng, :].rearrange("p t b (c i) -> p t b c i", i=4).rearrange("p t b c i -> p (b c) t i"),
-                scalar1=1.0 / (V * V),
-            )
-            st[("wg", c)] = wg
-
         def w_quant(c):
             ng = SIZES[c]
-            flat = st[("wg", c)][:].rearrange("p c t -> p (c t)")
+            flat = st[("wg", c)]
             wq = wq_ring[c % RING]
             wp = wp_ring[c % RING]
             runs = [(0, 1)] + [(g, g + 2) for g in range(1, ng - 1, 2)] + [(ng - 1, ng)]
@@ -177,15 +190,15 @@ def tile_garnetlayer_kernel(tc, fi_v, d_av, out):
             st[("acc", c)] = acc
 
         def finish(c):
-            lo, hi = split(c)
+            npairs = SIZES[c] // 2
             acc = st[("acc", c)]
-            wbar = st[("wbar", c)]
+            wbar = st[("wbar", c // 2)]
+            col = first_col(c)
             res = results.tile([P, PAIRS, N], F32, name="res")
-            for i in range(hi):
-                nc.scalar.activation(out=res[:, i, :], in_=acc[:, i, :], func=ACT.Copy, scale=wbar[:, i:i + 1])
-            queue = nc.sync if c >= nchunks - LATE else nc.gpsimd
+            for i in range(npairs):
+                nc.scalar.activation(out=res[:, i, :], in_=acc[:, i, :], func=ACT.Copy, scale=wbar[:, col + i:col + i + 1])
             i0 = starts[c] // 2
-            queue.dma_start(out=out_view[:, i0:i0 + hi, :], in_=res[:, 0:hi, :])
+            nc.sync.dma_start(out=out_view[:, i0:i0 + npairs, :], in_=res[:, 0:npairs, :])
 
         for c in range(AHEAD):
             load(c)
@@ -202,30 +215,33 @@ def tile_garnetlayer_kernel(tc, fi_v, d_av, out):
             wq_ring.append(wq)
             wp_ring.append(wp)
 
-        for t in range(nchunks + 2):
+        def live(c):
+            return 0 <= c < nchunks
+
+        for t in range(nchunks + 4):
             if t + AHEAD < nchunks:
                 load(t + AHEAD)
-            if t < nchunks:
-                weights(t)
-            new = t if t < nchunks else None
-            old = t - 1 if 0 <= t - 1 < nchunks else None
-            if old is not None:
-                w_sum(old)
-                w_reduce_scalar(old)
-            parts = pieces(new) if new is not None else []
-            if new is not None:
-                fi_tiles(new)
-                fi_regroup(new, parts[0][0], parts[0][1])
-            if old is not None:
-                w_cast(old)
-            for a, b in parts[1:]:
-                fi_regroup(new, a, b)
-            if old is not None:
-                w_quant(old)
-            for a, b in parts:
-                fi_quant(new, a, b)
-            if old is not None:
-                w_reduce_vector(old)
-                mx(old)
-            if t >= 2:
-                finish(t - 2)
+            if live(t - 2):
+                exp(t - 2)
+            if live(t - 3):
+                turn_back(t - 3)
+            if live(t - 4):
+                mx(t - 4)
+            if live(t - 1):
+                turn(t - 1)
+            if live(t):
+                square(t)
+                fi_tiles(t)
+                for a, b in pieces(t):
+                    fi_regroup(t, a, b)
+            if live(t - 3):
+                w_group(t - 3)
+            if live(t):
+                for a, b in pieces(t):
+                    fi_quant(t, a, b)
+            if live(t - 3):
+                w_quant(t - 3)
+            if live(t - 4):
+                if (t - 4) % 2 == 0:
+                    scale_sums(t - 4)
+                finish(t - 4)

@@ -22,6 +22,7 @@ PIECE = 4
 RING = 3
 UNIT = S
 AHEAD = 6
+LAG = 2
 SIZES = (2, 2, 4) + (8,) * 14 + (4, 2, 2)
 
 
@@ -50,18 +51,24 @@ def tile_garnetlayer_kernel(tc, fi_v, d_av, out):
 
         st = {}
 
+        def live(c):
+            return 0 <= c < nchunks
+
         def pieces(c):
             return [(a, min(a + PIECE, SIZES[c])) for a in range(0, SIZES[c], PIECE)]
 
-        def load(c):
+        def load_d(c):
             d_raw = loads.tile([P, G, PACK * S], BF16, name="d_raw")
-            fi_raw = loads.tile([P, G, PACK * N], BF16, name="fi_raw")
             g0 = starts[c]
             for a, b in pieces(c):
                 nc.sync.dma_start(out=d_raw[:, a:b, :], in_=d_view[:, g0 + a:g0 + b, :])
+            st[("d_raw", c)] = d_raw
+
+        def load_fi(c):
+            fi_raw = loads.tile([P, G, PACK * N], BF16, name="fi_raw")
+            g0 = starts[c]
             for a, b in pieces(c):
                 nc.sync.dma_start(out=fi_raw[:, a:b, :], in_=fi_view[:, g0 + a:g0 + b, :])
-            st[("d_raw", c)] = d_raw
             st[("fi_raw", c)] = fi_raw
 
         def square(c):
@@ -200,6 +207,12 @@ def tile_garnetlayer_kernel(tc, fi_v, d_av, out):
             i0 = starts[c] // 2
             nc.sync.dma_start(out=out_view[:, i0:i0 + npairs, :], in_=res[:, 0:npairs, :])
 
+        def load(c):
+            if live(c):
+                load_d(c)
+            if live(c - LAG):
+                load_fi(c - LAG)
+
         for c in range(AHEAD):
             load(c)
 
@@ -215,12 +228,8 @@ def tile_garnetlayer_kernel(tc, fi_v, d_av, out):
             wq_ring.append(wq)
             wp_ring.append(wp)
 
-        def live(c):
-            return 0 <= c < nchunks
-
         for t in range(nchunks + 4):
-            if t + AHEAD < nchunks:
-                load(t + AHEAD)
+            load(t + AHEAD)
             if live(t - 2):
                 exp(t - 2)
             if live(t - 3):
@@ -231,14 +240,16 @@ def tile_garnetlayer_kernel(tc, fi_v, d_av, out):
                 turn(t - 1)
             if live(t):
                 square(t)
-                fi_tiles(t)
-                for a, b in pieces(t):
-                    fi_regroup(t, a, b)
+            new = t - LAG
+            if live(new):
+                fi_tiles(new)
+                for a, b in pieces(new):
+                    fi_regroup(new, a, b)
             if live(t - 3):
                 w_group(t - 3)
-            if live(t):
-                for a, b in pieces(t):
-                    fi_quant(t, a, b)
+            if live(new):
+                for a, b in pieces(new):
+                    fi_quant(new, a, b)
             if live(t - 3):
                 w_quant(t - 3)
             if live(t - 4):

@@ -22,7 +22,7 @@ PIECE = 4
 RING = 3
 UNIT = S
 AHEAD = 6
-LAG = 2
+LAG = 1
 SIZES = (2, 2, 4) + (8,) * 14 + (4, 2, 2)
 
 
@@ -93,30 +93,17 @@ def tile_garnetlayer_kernel(tc, fi_v, d_av, out):
 
         def exp(c):
             wt = turned.tile([P, PAIRS, 2, P, 2], BF16, name="wt", align_bytes=64)
-            if c % 2 == 0:
-                wsum = keep.tile([P, 2 * PAIRS], F32, name="wsum")
-                wbar = keep.tile([P, 2 * PAIRS], F32, name="wbar")
-                st[("wsum", c // 2)] = wsum
-                st[("wbar", c // 2)] = wbar
-            wsum = st[("wsum", c // 2)]
-            col = first_col(c)
+            wsum = keep.tile([P, PAIRS], F32, name="wsum")
             for i in range(SIZES[c] // 2):
                 nc.scalar.activation(
                     out=wt[:, i],
                     in_=st[("dt", c, i)][:].rearrange("m (h e) q -> m h q e", e=2),
                     func=ACT.Exp,
                     scale=-1.0,
-                    accum_out=wsum[:, col + i:col + i + 1],
+                    accum_out=wsum[:, i:i + 1],
                 )
             st[("wt", c)] = wt
-
-        def first_col(c):
-            return 0 if c % 2 == 0 else SIZES[c - 1] // 2
-
-        def scale_sums(c):
-            last = c + 1 if c + 1 < nchunks else c
-            used = first_col(last) + SIZES[last] // 2
-            nc.scalar.mul(st[("wbar", c // 2)][:, 0:used], st[("wsum", c // 2)][:, 0:used], 1.0 / (V * V))
+            st[("wsum", c)] = wsum
 
         def turn_back(c):
             wt = st[("wt", c)]
@@ -130,16 +117,19 @@ def tile_garnetlayer_kernel(tc, fi_v, d_av, out):
                         )
                 st[("wb", c, k)] = wb
 
-        def w_group(c):
+        def on_scalar(c, k):
+            return k == 0 or c % 2 == 1
+
+        def w_group_tile(c):
+            st[("wg", c)] = work.tile([P, G * S * PACK], BF16, name="wg", align_bytes=64)
+
+        def w_group(c, copy, scalar):
             npairs = SIZES[c] // 2
-            wg = work.tile([P, G * S * PACK], BF16, name="wg", align_bytes=64)
-            words = wg[:].bitcast(F32).rearrange("p (i m h) -> p i m h", m=P, h=2)
+            words = st[("wg", c)][:].bitcast(F32).rearrange("p (i m h) -> p i m h", m=P, h=2)
             for k in range(0, npairs, 2):
                 hi = min(k + 2, npairs)
-                nc.vector.tensor_copy(
-                    out=words[:, k:hi], in_=st[("wb", c, k)][:, 0:hi - k].rearrange("p i h m -> p i m h")
-                )
-            st[("wg", c)] = wg
+                if on_scalar(c, k) == scalar:
+                    copy(out=words[:, k:hi], in_=st[("wb", c, k)][:, 0:hi - k].rearrange("p i h m -> p i m h"))
 
         def fi_tiles(c):
             st[("fg", c)] = work.tile([P, G, N, PACK], BF16, name="fg", align_bytes=64)
@@ -199,11 +189,16 @@ def tile_garnetlayer_kernel(tc, fi_v, d_av, out):
         def finish(c):
             npairs = SIZES[c] // 2
             acc = st[("acc", c)]
-            wbar = st[("wbar", c // 2)]
-            col = first_col(c)
+            wsum = st[("wsum", c)]
             res = results.tile([P, PAIRS, N], F32, name="res")
-            for i in range(npairs):
-                nc.scalar.activation(out=res[:, i, :], in_=acc[:, i, :], func=ACT.Copy, scale=wbar[:, col + i:col + i + 1])
+            nc.vector.scalar_tensor_tensor(
+                out=res[:, 0:npairs, :],
+                in0=acc[:, 0:npairs, :],
+                scalar=1.0 / (V * V),
+                in1=wsum[:, 0:npairs].unsqueeze(2).to_broadcast([P, npairs, N]),
+                op0=mybir.AluOpType.mult,
+                op1=mybir.AluOpType.mult,
+            )
             i0 = starts[c] // 2
             nc.sync.dma_start(out=out_view[:, i0:i0 + npairs, :], in_=res[:, 0:npairs, :])
 
@@ -238,6 +233,9 @@ def tile_garnetlayer_kernel(tc, fi_v, d_av, out):
                 mx(t - 4)
             if live(t - 1):
                 turn(t - 1)
+            if live(t - 3):
+                w_group_tile(t - 3)
+                w_group(t - 3, nc.scalar.copy, True)
             if live(t):
                 square(t)
             new = t - LAG
@@ -246,13 +244,11 @@ def tile_garnetlayer_kernel(tc, fi_v, d_av, out):
                 for a, b in pieces(new):
                     fi_regroup(new, a, b)
             if live(t - 3):
-                w_group(t - 3)
+                w_group(t - 3, nc.vector.tensor_copy, False)
             if live(new):
                 for a, b in pieces(new):
                     fi_quant(new, a, b)
             if live(t - 3):
                 w_quant(t - 3)
             if live(t - 4):
-                if (t - 4) % 2 == 0:
-                    scale_sums(t - 4)
                 finish(t - 4)

from contextlib import ExitStack

import concourse.mybir as mybir
from concourse.masks import make_identity

F32 = mybir.dt.float32
BF16 = mybir.dt.bfloat16
U32 = mybir.dt.uint32
U8 = mybir.dt.uint8
I32 = mybir.dt.int32
FP8X4 = mybir.dt.float8_e4m3fn_x4
ACT = mybir.ActivationFunctionType

B, V, S, N = 128, 512, 64, 128
P = 128
PACK = 4
FLOPS = 2 * B * V * S * N

G = 8
PAIRS = G // 2
PIECE = 4
RING = 3
UNIT = S
AHEAD = 6
LAG = 1
SIZES = (2, 2, 4) + (8,) * 14 + (4, 2, 2)


def tile_garnetlayer_kernel(tc, fi_v, d_av, out):
    nc = tc.nc
    fi_view = fi_v.rearrange("b (p j) n -> p b (j n)", j=PACK)
    d_view = d_av.rearrange("b (p j) s -> p b (j s)", j=PACK)
    out_view = out.rearrange("b (s n) -> (b s) n", n=N).rearrange("(i m) n -> m i n", m=P)
    nchunks = len(SIZES)
    starts = [sum(SIZES[:c]) for c in range(nchunks)]
    assert sum(SIZES) == B

    with ExitStack() as ctx:
        const = ctx.enter_context(tc.tile_pool(name="const", bufs=1))
        loads = ctx.enter_context(tc.tile_pool(name="loads", bufs=AHEAD + 2))
        work = ctx.enter_context(tc.tile_pool(name="work", bufs=2))
        turned = ctx.enter_context(tc.tile_pool(name="turned", bufs=3))
        keep = ctx.enter_context(tc.tile_pool(name="keep", bufs=4))
        codes = ctx.enter_context(tc.tile_pool(name="codes", bufs=6))
        results = ctx.enter_context(tc.tile_pool(name="results", bufs=8))
        psum_d = ctx.enter_context(tc.psum_pool(name="psum_d", bufs=4))
        psum_w = ctx.enter_context(tc.psum_pool(name="psum_w", bufs=2))
        psum_hi = ctx.enter_context(tc.psum_pool(name="psum_hi", bufs=2))

        ctx.enter_context(tc.manual_schedule())

        st = {}

        def live(c):
            return 0 <= c < nchunks

        def pieces(c):
            return [(a, min(a + PIECE, SIZES[c])) for a in range(0, SIZES[c], PIECE)]

        def load_d(c):
            d_raw = loads.tile([P, G, PACK * S], BF16, name="d_raw")
            g0 = starts[c]
            for a, b in pieces(c):
                nc.sync.dma_start(out=d_raw[:, a:b, :], in_=d_view[:, g0 + a:g0 + b, :])
            st[("d_raw", c)] = d_raw

        def load_fi(c):
            fi_raw = loads.tile([P, G, PACK * N], BF16, name="fi_raw")
            g0 = starts[c]
            for a, b in pieces(c):
                nc.sync.dma_start(out=fi_raw[:, a:b, :], in_=fi_view[:, g0 + a:g0 + b, :])
            st[("fi_raw", c)] = fi_raw

        def square(c):
            ng = SIZES[c]
            dsq = turned.tile([P, PACK, G, S], F32, name="dsq")
            nc.scalar.activation(
                out=dsq[:, :, 0:ng, :],
                in_=st[("d_raw", c)][:, 0:ng, :].rearrange("p b (j s) -> p j b s", j=PACK),
                func=ACT.Square,
            )
            st[("dsq", c)] = dsq

        def turn(c):
            dsq = st[("dsq", c)]
            for i in range(SIZES[c] // 2):
                dt = psum_d.tile([P, PACK, P], F32, name="dt")
                for j in range(PACK):
                    nc.tensor.transpose(
                        dt[:, j, :], dsq[:, j, 2 * i:2 * i + 2, :].rearrange("p b s -> p (b s)"), ident[:]
                    )
                st[("dt", c, i)] = dt

        def exp(c):
            wt = turned.tile([P, PAIRS, 2, P, 2], BF16, name="wt", align_bytes=64)
            wsum = keep.tile([P, PAIRS], F32, name="wsum")
            for i in range(SIZES[c] // 2):
                nc.scalar.activation(
                    out=wt[:, i],
                    in_=st[("dt", c, i)][:].rearrange("m (h e) q -> m h q e", e=2),
                    func=ACT.Exp,
                    scale=-1.0,
                    accum_out=wsum[:, i:i + 1],
                )
            st[("wt", c)] = wt
            st[("wsum", c)] = wsum

        def turn_back(c):
            wt = st[("wt", c)]
            npairs = SIZES[c] // 2
            for k in range(0, npairs, 2):
                wb = psum_w.tile([P, 2, 2, P], F32, name="wb")
                for i in range(k, min(k + 2, npairs)):
                    for h in range(2):
                        nc.tensor.transpose(
                            wb[:, i - k, h, :], wt[:, i, h].rearrange("m q e -> m (q e)").bitcast(F32), ident[:]
                        )
                st[("wb", c, k)] = wb

        def on_scalar(c, k):
            return k == 0 or c % 2 == 1

        def w_group_tile(c):
            st[("wg", c)] = work.tile([P, G * S * PACK], BF16, name="wg", align_bytes=64)

        def w_group(c, copy, scalar):
            npairs = SIZES[c] // 2
            words = st[("wg", c)][:].bitcast(F32).rearrange("p (i m h) -> p i m h", m=P, h=2)
            for k in range(0, npairs, 2):
                hi = min(k + 2, npairs)
                if on_scalar(c, k) == scalar:
                    copy(out=words[:, k:hi], in_=st[("wb", c, k)][:, 0:hi - k].rearrange("p i h m -> p i m h"))

        def fi_tiles(c):
            st[("fg", c)] = work.tile([P, G, N, PACK], BF16, name="fg", align_bytes=64)
            st[("fq", c)] = codes.tile([P, G * N], U32, name="fq", align_bytes=64)
            st[("fp", c)] = codes.tile([P, G * N], U8, name="fp", align_bytes=64)

        def fi_regroup(c, a, b):
            nc.vector.tensor_copy(
                out=st[("fg", c)][:, a:b].rearrange("p b (c i) t -> p b c t i", i=4),
                in_=st[("fi_raw", c)][:, a:b, :].rearrange("p b (t c i) -> p b c t i", t=PACK, i=4),
            )

        def fi_quant(c, a, b):
            cols = slice(a * N, b * N)
            nc.vector.quantize_mx(
                out=st[("fq", c)][:, cols].bitcast(FP8X4),
                scales=st[("fp", c)][:, cols],
                in_=st[("fg", c)][:, a:b].rearrange("p b n t -> p (b n t)"),
            )

        def w_quant(c):
            ng = SIZES[c]
            flat = st[("wg", c)]
            wq = wq_ring[c % RING]
            wp = wp_ring[c % RING]
            runs = [(0, 1)] + [(g, g + 2) for g in range(1, ng - 1, 2)] + [(ng - 1, ng)]
            for lo, hi in runs:
                unit = 3 * (lo // 2) + 2 * (lo % 2)
                cols = slice(unit * UNIT, (unit + hi - lo) * UNIT)
                nc.vector.quantize_mx(
                    out=wq[:, cols].bitcast(FP8X4),
                    scales=wp[:, cols],
                    in_=flat[:, lo * S * PACK:hi * S * PACK],
                )

        def mx(c):
            wq = wq_ring[c % RING]
            wp = wp_ring[c % RING]
            fq = st[("fq", c)]
            fp = st[("fp", c)]
            acc = psum_hi.tile([P, PAIRS, N], F32, name="acc")
            for i in range(SIZES[c] // 2):
                for odd in range(2):
                    wcols = slice((3 * i + odd) * UNIT, (3 * i + odd + 2) * UNIT)
                    fcols = slice((2 * i + odd) * N, (2 * i + odd + 1) * N)
                    nc.tensor.matmul_mx(
                        out=acc[:, i, :],
                        lhsT=wq[:, wcols].bitcast(FP8X4),
                        lhsT_scale=wp[:, wcols],
                        rhs=fq[:, fcols].bitcast(FP8X4),
                        rhs_scale=fp[:, fcols],
                        start=(odd == 0),
                        stop=(odd == 1),
                    )
            st[("acc", c)] = acc

        def finish(c):
            npairs = SIZES[c] // 2
            acc = st[("acc", c)]
            wsum = st[("wsum", c)]
            res = results.tile([P, PAIRS, N], F32, name="res")
            nc.vector.scalar_tensor_tensor(
                out=res[:, 0:npairs, :],
                in0=acc[:, 0:npairs, :],
                scalar=1.0 / (V * V),
                in1=wsum[:, 0:npairs].unsqueeze(2).to_broadcast([P, npairs, N]),
                op0=mybir.AluOpType.mult,
                op1=mybir.AluOpType.mult,
            )
            i0 = starts[c] // 2
            nc.sync.dma_start(out=out_view[:, i0:i0 + npairs, :], in_=res[:, 0:npairs, :])

        def load(c):
            if live(c):
                load_d(c)
            if live(c - LAG):
                load_fi(c - LAG)

        for c in range(AHEAD):
            load(c)

        ident = const.tile([P, P], F32, name="ident")
        make_identity(nc, ident[:])
        wq_ring = []
        wp_ring = []
        for r in range(RING):
            wq = const.tile([P, 3 * PAIRS * UNIT], U32, name="wq%d" % r, align_bytes=64)
            wp = const.tile([P, 3 * PAIRS * UNIT], U8, name="wp%d" % r, align_bytes=64)
            nc.vector.memset(wq[:].bitcast(I32).rearrange("p (i u w) -> p i u w", u=3, w=UNIT)[:, :, 1, :], 0)
            nc.vector.memset(wp[:].bitcast(I32).rearrange("p (i u w) -> p i u w", u=3, w=UNIT // 4)[:, :, 1, :], 0)
            wq_ring.append(wq)
            wp_ring.append(wp)

        for t in range(nchunks + 4):
            load(t + AHEAD)
            if live(t - 2):
                exp(t - 2)
            if live(t - 3):
                turn_back(t - 3)
            if live(t - 4):
                mx(t - 4)
            if live(t - 1):
                turn(t - 1)
            if live(t - 3):
                w_group_tile(t - 3)
                w_group(t - 3, nc.scalar.copy, True)
            if live(t):
                square(t)
            new = t - LAG
            if live(new):
                fi_tiles(new)
                for a, b in pieces(new):
                    fi_regroup(new, a, b)
            if live(t - 3):
                w_group(t - 3, nc.vector.tensor_copy, False)
            if live(new):
                for a, b in pieces(new):
                    fi_quant(new, a, b)
            if live(t - 3):
                w_quant(t - 3)
            if live(t - 4):
                finish(t - 4)
